import numpy as np
import ml_dtypes

BF16 = ml_dtypes.bfloat16


def bf(x):
    return np.asarray(x, np.float32).astype(BF16)


def f32(x):
    return np.asarray(x, np.float32)


def f64(x):
    return np.asarray(x).astype(np.float64)


def striped(idx):
    return np.tile(idx.reshape(-1, 16).T, (8, 1))


C, S, N = 128, 4096, 1024
SIG = 2.0


def setup_inputs():
    return {"base": f32(np.random.standard_normal((C, S))), "x": bf(np.random.standard_normal((N, C))), "rate": bf(np.exp(SIG * np.random.standard_normal((N, N))) / N), "offs": striped(np.random.permutation(S)[:N])}


def reference(base, x, rate, offs):
    idx = offs[:16].T.reshape(-1)
    num = f64(x).T @ f64(rate)
    s = np.sum(f64(rate), axis=0, keepdims=True)
    out = f64(base).copy()
    out[:, idx] = num * (1.0 / s)
    return out

@@ -1,0 +1,60 @@
+import concourse.mybir as mybir
+
+P = 128
+S = 4096
+N = 1024
+ROWS = N // P
+BANK = 512
+HALVES = N // BANK
+FLOPS = 2 * P * N * N + N * N
+
+BF16, F32, U16 = mybir.dt.bfloat16, mybir.dt.float32, mybir.dt.uint16
+
+
+def tile_som_kernel(tc, base, x, rate, offs, out):
+    nc = tc.nc
+    with (
+        tc.tile_pool(name="held", bufs=1) as held,
+        tc.psum_pool(name="psum", bufs=1) as psum,
+    ):
+        offsets = held.tile([P, N // 16], U16, name="offsets")
+        nc.sync.dma_start(offsets[:], offs)
+
+        x_sb = held.tile([P, ROWS, P], BF16, name="x_sb")
+        nc.sync.dma_start(x_sb[:], x.rearrange("(p r) c -> p r c", r=ROWS))
+        rate_view = rate.rearrange("(p r) j -> p r j", r=ROWS)
+        rate_sb = []
+        for pair in range(ROWS // 2):
+            rate_pair = held.tile([P, 2, N], BF16, name=f"rate{pair}")
+            nc.sync.dma_start(rate_pair[:], rate_view[:, 2 * pair : 2 * pair + 2, :])
+            rate_sb.append(rate_pair)
+
+        window = held.tile([P, S], F32, name="window")
+        for quarter in range(4):
+            cols = slice(quarter * (S // 4), (quarter + 1) * (S // 4))
+            nc.sync.dma_start(window[:, cols], base[:, cols])
+
+        ones = held.tile([P, P], BF16, name="ones")
+        nc.vector.memset(ones[:], 1.0)
+
+        num_ps = [psum.tile([P, BANK], F32, name=f"num_ps{h}") for h in range(HALVES)]
+        sum_ps = [psum.tile([P, BANK], F32, name=f"sum_ps{h}") for h in range(HALVES)]
+        for r in range(ROWS):
+            first, last = r == 0, r == ROWS - 1
+            for h in range(HALVES):
+                moving = rate_sb[r // 2][:, r % 2, h * BANK : (h + 1) * BANK]
+                nc.tensor.matmul(sum_ps[h][:], ones[:], moving, start=first, stop=last)
+                nc.tensor.matmul(num_ps[h][:], x_sb[:, r, :], moving, start=first, stop=last)
+
+        recip = held.tile([P, N], F32, name="recip")
+        num = held.tile([P, N], F32, name="num")
+        for h in range(HALVES):
+            cols = slice(h * BANK, (h + 1) * BANK)
+            nc.vector.reciprocal(recip[:, cols], sum_ps[h][:])
+            nc.scalar.copy(num[:, cols], num_ps[h][:])
+
+        nc.vector.tensor_tensor(window[:].indirect(offsets[:]), num[:], recip[:], mybir.AluOpType.mult)
+
+        for quarter in range(4):
+            cols = slice(quarter * (S // 4), (quarter + 1) * (S // 4))
+            nc.sync.dma_start(out[:, cols], window[:, cols])

@@ -1,9 +1,11 @@
 import concourse.mybir as mybir
+from concourse.masks import make_identity
 
 P = 128
 S = 4096
 N = 1024
 ROWS = N // P
+BLOCKS = N // P
 BANK = 512
 HALVES = N // BANK
 FLOPS = 2 * P * N * N + N * N
@@ -34,24 +36,44 @@ def tile_som_kernel(tc, base, x, rate, offs, out):
             cols = slice(quarter * (S // 4), (quarter + 1) * (S // 4))
             nc.sync.dma_start(window[:, cols], base[:, cols])
 
-        ones = held.tile([P, P], BF16, name="ones")
-        nc.vector.memset(ones[:], 1.0)
+        one_col = held.tile([P, 1], BF16, name="one_col")
+        nc.vector.memset(one_col[:], 1.0)
+        identity = held.tile([P, P], F32, name="identity")
+        make_identity(nc, identity[:])
 
         num_ps = [psum.tile([P, BANK], F32, name=f"num_ps{h}") for h in range(HALVES)]
-        sum_ps = [psum.tile([P, BANK], F32, name=f"sum_ps{h}") for h in range(HALVES)]
+        part_ps = psum.tile([P, BLOCKS, ROWS], F32, name="part_ps")
         for r in range(ROWS):
-            first, last = r == 0, r == ROWS - 1
+            rate_r = rate_sb[r // 2][:, r % 2, :]
+            for b in range(BLOCKS):
+                nc.tensor.matmul(
+                    part_ps[:, b, r : r + 1], rate_r[:, b * P : (b + 1) * P], one_col[:], start=True, stop=True
+                )
             for h in range(HALVES):
-                moving = rate_sb[r // 2][:, r % 2, h * BANK : (h + 1) * BANK]
-                nc.tensor.matmul(sum_ps[h][:], ones[:], moving, start=first, stop=last)
-                nc.tensor.matmul(num_ps[h][:], x_sb[:, r, :], moving, start=first, stop=last)
+                nc.tensor.matmul(
+                    num_ps[h][:],
+                    x_sb[:, r, :],
+                    rate_r[:, h * BANK : (h + 1) * BANK],
+                    start=(r == 0),
+                    stop=(r == ROWS - 1),
+                )
 
-        recip = held.tile([P, N], F32, name="recip")
+        s_t = held.tile([P, BLOCKS], F32, name="s_t")
+        nc.vector.reduce_sum(s_t[:], part_ps[:], axis=mybir.AxisListType.X)
+        recip_t = held.tile([P, BLOCKS], F32, name="recip_t")
+        nc.vector.reciprocal(recip_t[:], s_t[:])
+
+        recip_ps = [psum.tile([P, BANK], F32, name=f"recip_ps{h}") for h in range(HALVES)]
+        for b in range(BLOCKS):
+            h, q = divmod(b * P, BANK)
+            nc.tensor.transpose(recip_ps[h][:, q : q + P], recip_t[:, b : b + 1].to_broadcast([P, P]), identity[:])
+
         num = held.tile([P, N], F32, name="num")
+        recip = held.tile([P, N], F32, name="recip")
         for h in range(HALVES):
             cols = slice(h * BANK, (h + 1) * BANK)
-            nc.vector.reciprocal(recip[:, cols], sum_ps[h][:])
             nc.scalar.copy(num[:, cols], num_ps[h][:])
+            nc.vector.tensor_copy(recip[:, cols], recip_ps[h][:])
 
         nc.vector.tensor_tensor(window[:].indirect(offsets[:]), num[:], recip[:], mybir.AluOpType.mult)
 

@@ -41,21 +41,15 @@ def tile_som_kernel(tc, base, x, rate, offs, out):
         identity = held.tile([P, P], F32, name="identity")
         make_identity(nc, identity[:])
 
-        num_ps = [psum.tile([P, BANK], F32, name=f"num_ps{h}") for h in range(HALVES)]
         part_ps = psum.tile([P, BLOCKS, ROWS], F32, name="part_ps")
         for r in range(ROWS):
-            rate_r = rate_sb[r // 2][:, r % 2, :]
             for b in range(BLOCKS):
                 nc.tensor.matmul(
-                    part_ps[:, b, r : r + 1], rate_r[:, b * P : (b + 1) * P], one_col[:], start=True, stop=True
-                )
-            for h in range(HALVES):
-                nc.tensor.matmul(
-                    num_ps[h][:],
-                    x_sb[:, r, :],
-                    rate_r[:, h * BANK : (h + 1) * BANK],
-                    start=(r == 0),
-                    stop=(r == ROWS - 1),
+                    part_ps[:, b, r : r + 1],
+                    rate_sb[r // 2][:, r % 2, b * P : (b + 1) * P],
+                    one_col[:],
+                    start=True,
+                    stop=True,
                 )
 
         s_t = held.tile([P, BLOCKS], F32, name="s_t")
@@ -64,16 +58,22 @@ def tile_som_kernel(tc, base, x, rate, offs, out):
         nc.vector.reciprocal(recip_t[:], s_t[:])
 
         recip_ps = [psum.tile([P, BANK], F32, name=f"recip_ps{h}") for h in range(HALVES)]
+        recip = held.tile([P, N], F32, name="recip")
         for b in range(BLOCKS):
             h, q = divmod(b * P, BANK)
             nc.tensor.transpose(recip_ps[h][:, q : q + P], recip_t[:, b : b + 1].to_broadcast([P, P]), identity[:])
+        for h in range(HALVES):
+            nc.vector.tensor_copy(recip[:, h * BANK : (h + 1) * BANK], recip_ps[h][:])
 
+        num_ps = [psum.tile([P, BANK], F32, name=f"num_ps{h}") for h in range(HALVES)]
         num = held.tile([P, N], F32, name="num")
-        recip = held.tile([P, N], F32, name="recip")
         for h in range(HALVES):
             cols = slice(h * BANK, (h + 1) * BANK)
+            for r in range(ROWS):
+                nc.tensor.matmul(
+                    num_ps[h][:], x_sb[:, r, :], rate_sb[r // 2][:, r % 2, cols], start=(r == 0), stop=(r == ROWS - 1)
+                )
             nc.scalar.copy(num[:, cols], num_ps[h][:])
-            nc.vector.tensor_copy(recip[:, cols], recip_ps[h][:])
 
         nc.vector.tensor_tensor(window[:].indirect(offsets[:]), num[:], recip[:], mybir.AluOpType.mult)
 

@@ -19,17 +19,15 @@ def tile_som_kernel(tc, base, x, rate, offs, out):
         tc.tile_pool(name="held", bufs=1) as held,
         tc.psum_pool(name="psum", bufs=1) as psum,
     ):
-        offsets = held.tile([P, N // 16], U16, name="offsets")
-        nc.sync.dma_start(offsets[:], offs)
-
-        x_sb = held.tile([P, ROWS, P], BF16, name="x_sb")
-        nc.sync.dma_start(x_sb[:], x.rearrange("(p r) c -> p r c", r=ROWS))
         rate_view = rate.rearrange("(p r) j -> p r j", r=ROWS)
-        rate_sb = []
-        for pair in range(ROWS // 2):
-            rate_pair = held.tile([P, 2, N], BF16, name=f"rate{pair}")
-            nc.sync.dma_start(rate_pair[:], rate_view[:, 2 * pair : 2 * pair + 2, :])
-            rate_sb.append(rate_pair)
+        rate_sb = [held.tile([P, N], BF16, name=f"rate{r}") for r in range(ROWS)]
+        x_sb = held.tile([P, ROWS, P], BF16, name="x_sb")
+        offsets = held.tile([P, N // 16], U16, name="offsets")
+        nc.sync.dma_start(rate_sb[0][:], rate_view[:, 0, :])
+        nc.sync.dma_start(x_sb[:], x.rearrange("(p r) c -> p r c", r=ROWS))
+        for r in range(1, ROWS):
+            nc.sync.dma_start(rate_sb[r][:], rate_view[:, r, :])
+        nc.sync.dma_start(offsets[:], offs)
 
         window = held.tile([P, S], F32, name="window")
         for quarter in range(4):
@@ -46,7 +44,7 @@ def tile_som_kernel(tc, base, x, rate, offs, out):
             for b in range(BLOCKS):
                 nc.tensor.matmul(
                     part_ps[:, b, r : r + 1],
-                    rate_sb[r // 2][:, r % 2, b * P : (b + 1) * P],
+                    rate_sb[r][:, b * P : (b + 1) * P],
                     one_col[:],
                     start=True,
                     stop=True,
@@ -71,7 +69,7 @@ def tile_som_kernel(tc, base, x, rate, offs, out):
             cols = slice(h * BANK, (h + 1) * BANK)
             for r in range(ROWS):
                 nc.tensor.matmul(
-                    num_ps[h][:], x_sb[:, r, :], rate_sb[r // 2][:, r % 2, cols], start=(r == 0), stop=(r == ROWS - 1)
+                    num_ps[h][:], x_sb[:, r, :], rate_sb[r][:, cols], start=(r == 0), stop=(r == ROWS - 1)
                 )
             nc.scalar.copy(num[:, cols], num_ps[h][:])
 

@@ -8,6 +8,7 @@ ROWS = N // P
 BLOCKS = N // P
 BANK = 512
 HALVES = N // BANK
+WARM_UP = 4
 FLOPS = 2 * P * N * N + N * N
 
 BF16, F32, U16 = mybir.dt.bfloat16, mybir.dt.float32, mybir.dt.uint16
@@ -21,18 +22,26 @@ def tile_som_kernel(tc, base, x, rate, offs, out):
     ):
         rate_view = rate.rearrange("(p r) j -> p r j", r=ROWS)
         rate_sb = [held.tile([P, N], BF16, name=f"rate{r}") for r in range(ROWS)]
-        x_sb = held.tile([P, ROWS, P], BF16, name="x_sb")
+        x_view = x.rearrange("(p r) c -> p r c", r=ROWS)
+        x_sb = [held.tile([P, ROWS // 2, P], BF16, name=f"x{half}") for half in range(2)]
         offsets = held.tile([P, N // 16], U16, name="offsets")
         nc.sync.dma_start(rate_sb[0][:], rate_view[:, 0, :])
-        nc.sync.dma_start(x_sb[:], x.rearrange("(p r) c -> p r c", r=ROWS))
+        nc.sync.dma_start(x_sb[0][:], x_view[:, 0 : ROWS // 2, :])
         for r in range(1, ROWS):
             nc.sync.dma_start(rate_sb[r][:], rate_view[:, r, :])
+        nc.sync.dma_start(x_sb[1][:], x_view[:, ROWS // 2 : ROWS, :])
         nc.sync.dma_start(offsets[:], offs)
 
         window = held.tile([P, S], F32, name="window")
         for quarter in range(4):
             cols = slice(quarter * (S // 4), (quarter + 1) * (S // 4))
             nc.sync.dma_start(window[:, cols], base[:, cols])
+
+        zeros = held.tile([P, BANK], BF16, name="zeros")
+        nc.gpsimd.memset(zeros[:], 0.0)
+        idle_ps = psum.tile([P, BANK], F32, name="idle_ps")
+        for turn in range(WARM_UP):
+            nc.tensor.matmul(idle_ps[:], zeros[:, 0:P], zeros[:], start=True, stop=True)
 
         one_col = held.tile([P, 1], BF16, name="one_col")
         nc.vector.memset(one_col[:], 1.0)
@@ -69,9 +78,10 @@ def tile_som_kernel(tc, base, x, rate, offs, out):
             cols = slice(h * BANK, (h + 1) * BANK)
             for r in range(ROWS):
                 nc.tensor.matmul(
-                    num_ps[h][:], x_sb[:, r, :], rate_sb[r][:, cols], start=(r == 0), stop=(r == ROWS - 1)
+                    num_ps[h][:], x_sb[r // (ROWS // 2)][:, r % (ROWS // 2), :], rate_sb[r][:, cols], start=(r == 0), stop=(r == ROWS - 1)
                 )
-            nc.scalar.copy(num[:, cols], num_ps[h][:])
+        nc.scalar.copy(num[:, 0:BANK], num_ps[0][:])
+        nc.vector.tensor_copy(num[:, BANK:N], num_ps[1][:])
 
         nc.vector.tensor_tensor(window[:].indirect(offsets[:]), num[:], recip[:], mybir.AluOpType.mult)
 

@@ -8,7 +8,6 @@ ROWS = N // P
 BLOCKS = N // P
 BANK = 512
 HALVES = N // BANK
-WARM_UP = 4
 FLOPS = 2 * P * N * N + N * N
 
 BF16, F32, U16 = mybir.dt.bfloat16, mybir.dt.float32, mybir.dt.uint16
@@ -20,28 +19,20 @@ def tile_som_kernel(tc, base, x, rate, offs, out):
         tc.tile_pool(name="held", bufs=1) as held,
         tc.psum_pool(name="psum", bufs=1) as psum,
     ):
-        rate_view = rate.rearrange("(p r) j -> p r j", r=ROWS)
-        rate_sb = [held.tile([P, N], BF16, name=f"rate{r}") for r in range(ROWS)]
-        x_view = x.rearrange("(p r) c -> p r c", r=ROWS)
-        x_sb = [held.tile([P, ROWS // 2, P], BF16, name=f"x{half}") for half in range(2)]
         offsets = held.tile([P, N // 16], U16, name="offsets")
-        nc.sync.dma_start(rate_sb[0][:], rate_view[:, 0, :])
-        nc.sync.dma_start(x_sb[0][:], x_view[:, 0 : ROWS // 2, :])
-        for r in range(1, ROWS):
-            nc.sync.dma_start(rate_sb[r][:], rate_view[:, r, :])
-        nc.sync.dma_start(x_sb[1][:], x_view[:, ROWS // 2 : ROWS, :])
         nc.sync.dma_start(offsets[:], offs)
 
-        window = held.tile([P, S], F32, name="window")
-        for quarter in range(4):
-            cols = slice(quarter * (S // 4), (quarter + 1) * (S // 4))
-            nc.sync.dma_start(window[:, cols], base[:, cols])
+        x_sb = held.tile([P, ROWS, P], BF16, name="x_sb")
+        nc.sync.dma_start(x_sb[:], x.rearrange("(p r) c -> p r c", r=ROWS))
+        rate_view = rate.rearrange("(p r) j -> p r j", r=ROWS)
+        rate_sb = []
+        for pair in range(ROWS // 2):
+            rate_pair = held.tile([P, 2, N], BF16, name=f"rate{pair}")
+            nc.sync.dma_start(rate_pair[:], rate_view[:, 2 * pair : 2 * pair + 2, :])
+            rate_sb.append(rate_pair)
 
-        zeros = held.tile([P, BANK], BF16, name="zeros")
-        nc.gpsimd.memset(zeros[:], 0.0)
-        idle_ps = psum.tile([P, BANK], F32, name="idle_ps")
-        for turn in range(WARM_UP):
-            nc.tensor.matmul(idle_ps[:], zeros[:, 0:P], zeros[:], start=True, stop=True)
+        window = held.tile([P, S], F32, name="window")
+        nc.sync.dma_start(window[:], base)
 
         one_col = held.tile([P, 1], BF16, name="one_col")
         nc.vector.memset(one_col[:], 1.0)
@@ -53,7 +44,7 @@ def tile_som_kernel(tc, base, x, rate, offs, out):
             for b in range(BLOCKS):
                 nc.tensor.matmul(
                     part_ps[:, b, r : r + 1],
-                    rate_sb[r][:, b * P : (b + 1) * P],
+                    rate_sb[r // 2][:, r % 2, b * P : (b + 1) * P],
                     one_col[:],
                     start=True,
                     stop=True,
@@ -78,13 +69,10 @@ def tile_som_kernel(tc, base, x, rate, offs, out):
             cols = slice(h * BANK, (h + 1) * BANK)
             for r in range(ROWS):
                 nc.tensor.matmul(
-                    num_ps[h][:], x_sb[r // (ROWS // 2)][:, r % (ROWS // 2), :], rate_sb[r][:, cols], start=(r == 0), stop=(r == ROWS - 1)
+                    num_ps[h][:], x_sb[:, r, :], rate_sb[r // 2][:, r % 2, cols], start=(r == 0), stop=(r == ROWS - 1)
                 )
-        nc.scalar.copy(num[:, 0:BANK], num_ps[0][:])
-        nc.vector.tensor_copy(num[:, BANK:N], num_ps[1][:])
+            nc.scalar.copy(num[:, cols], num_ps[h][:])
 
         nc.vector.tensor_tensor(window[:].indirect(offsets[:]), num[:], recip[:], mybir.AluOpType.mult)
 
-        for quarter in range(4):
-            cols = slice(quarter * (S // 4), (quarter + 1) * (S // 4))
-            nc.sync.dma_start(out[:, cols], window[:, cols])
+        nc.sync.dma_start(out, window[:])

@@ -8,6 +8,7 @@ ROWS = N // P
 BLOCKS = N // P
 BANK = 512
 HALVES = N // BANK
+BLOCKS_IN_HALF = BANK // P
 FLOPS = 2 * P * N * N + N * N
 
 BF16, F32, U16 = mybir.dt.bfloat16, mybir.dt.float32, mybir.dt.uint16
@@ -40,6 +41,27 @@ def tile_som_kernel(tc, base, x, rate, offs, out):
         make_identity(nc, identity[:])
 
         part_ps = psum.tile([P, BLOCKS, ROWS], F32, name="part_ps")
+        num_ps = [psum.tile([P, BANK], F32, name=f"num_ps{h}") for h in range(HALVES)]
+        recip_ps = [psum.tile([P, BANK], F32, name=f"recip_ps{h}") for h in range(HALVES)]
+        num = [held.tile([P, BANK], F32, name=f"num{h}") for h in range(HALVES)]
+        recip = [held.tile([P, BANK], F32, name=f"recip{h}") for h in range(HALVES)]
+
+        def add_to_num(h, r):
+            nc.tensor.matmul(
+                num_ps[h][:],
+                x_sb[:, r, :],
+                rate_sb[r // 2][:, r % 2, h * BANK : (h + 1) * BANK],
+                start=(r == 0),
+                stop=(r == ROWS - 1),
+            )
+
+        def spread_recip(h):
+            for q in range(BLOCKS_IN_HALF):
+                b = h * BLOCKS_IN_HALF + q
+                nc.tensor.transpose(
+                    recip_ps[h][:, q * P : (q + 1) * P], recip_t[:, b : b + 1].to_broadcast([P, P]), identity[:]
+                )
+
         for r in range(ROWS):
             for b in range(BLOCKS):
                 nc.tensor.matmul(
@@ -49,30 +71,25 @@ def tile_som_kernel(tc, base, x, rate, offs, out):
                     start=True,
                     stop=True,
                 )
+            add_to_num(0, r)
 
         s_t = held.tile([P, BLOCKS], F32, name="s_t")
         nc.vector.reduce_sum(s_t[:], part_ps[:], axis=mybir.AxisListType.X)
         recip_t = held.tile([P, BLOCKS], F32, name="recip_t")
         nc.vector.reciprocal(recip_t[:], s_t[:])
 
-        recip_ps = [psum.tile([P, BANK], F32, name=f"recip_ps{h}") for h in range(HALVES)]
-        recip = held.tile([P, N], F32, name="recip")
-        for b in range(BLOCKS):
-            h, q = divmod(b * P, BANK)
-            nc.tensor.transpose(recip_ps[h][:, q : q + P], recip_t[:, b : b + 1].to_broadcast([P, P]), identity[:])
-        for h in range(HALVES):
-            nc.vector.tensor_copy(recip[:, h * BANK : (h + 1) * BANK], recip_ps[h][:])
+        nc.scalar.copy(num[0][:], num_ps[0][:])
+        spread_recip(0)
+        nc.vector.tensor_copy(recip[0][:], recip_ps[0][:])
 
-        num_ps = [psum.tile([P, BANK], F32, name=f"num_ps{h}") for h in range(HALVES)]
-        num = held.tile([P, N], F32, name="num")
-        for h in range(HALVES):
-            cols = slice(h * BANK, (h + 1) * BANK)
-            for r in range(ROWS):
-                nc.tensor.matmul(
-                    num_ps[h][:], x_sb[:, r, :], rate_sb[r // 2][:, r % 2, cols], start=(r == 0), stop=(r == ROWS - 1)
-                )
-            nc.scalar.copy(num[:, cols], num_ps[h][:])
+        spread_recip(1)
+        nc.scalar.copy(recip[1][:], recip_ps[1][:])
+        for r in range(ROWS):
+            add_to_num(1, r)
+        nc.scalar.copy(num[1][:], num_ps[1][:])
 
-        nc.vector.tensor_tensor(window[:].indirect(offsets[:]), num[:], recip[:], mybir.AluOpType.mult)
+        for h in range(HALVES):
+            piece = offsets[:, h * (BANK // 16) : (h + 1) * (BANK // 16)]
+            nc.vector.tensor_tensor(window[:].indirect(piece), num[h][:], recip[h][:], mybir.AluOpType.mult)
 
         nc.sync.dma_start(out, window[:])

@@ -40,8 +40,9 @@ def tile_som_kernel(tc, base, x, rate, offs, out):
         identity = held.tile([P, P], F32, name="identity")
         make_identity(nc, identity[:])
 
-        part_ps = psum.tile([P, BLOCKS, ROWS], F32, name="part_ps")
-        num_ps = [psum.tile([P, BANK], F32, name=f"num_ps{h}") for h in range(HALVES)]
+        part_bank = psum.tile([P, BANK], F32, name="part_bank", tag="shared_bank")
+        part_ps = part_bank[:, 0 : BLOCKS * ROWS].rearrange("p (b r) -> p b r", r=ROWS)
+        num_ps = [psum.tile([P, BANK], F32, name="num_ps0")]
         recip_ps = [psum.tile([P, BANK], F32, name=f"recip_ps{h}") for h in range(HALVES)]
         num = [held.tile([P, BANK], F32, name=f"num{h}") for h in range(HALVES)]
         recip = [held.tile([P, BANK], F32, name=f"recip{h}") for h in range(HALVES)]
@@ -74,7 +75,7 @@ def tile_som_kernel(tc, base, x, rate, offs, out):
             add_to_num(0, r)
 
         s_t = held.tile([P, BLOCKS], F32, name="s_t")
-        nc.vector.reduce_sum(s_t[:], part_ps[:], axis=mybir.AxisListType.X)
+        nc.vector.reduce_sum(s_t[:], part_ps, axis=mybir.AxisListType.X)
         recip_t = held.tile([P, BLOCKS], F32, name="recip_t")
         nc.vector.reciprocal(recip_t[:], s_t[:])
 
@@ -84,6 +85,7 @@ def tile_som_kernel(tc, base, x, rate, offs, out):
 
         spread_recip(1)
         nc.scalar.copy(recip[1][:], recip_ps[1][:])
+        num_ps.append(psum.tile([P, BANK], F32, name="num_ps1", tag="shared_bank"))
         for r in range(ROWS):
             add_to_num(1, r)
         nc.scalar.copy(num[1][:], num_ps[1][:])

@@ -9,6 +9,7 @@ BLOCKS = N // P
 BANK = 512
 HALVES = N // BANK
 BLOCKS_IN_HALF = BANK // P
+GROUP = 4
 FLOPS = 2 * P * N * N + N * N
 
 BF16, F32, U16 = mybir.dt.bfloat16, mybir.dt.float32, mybir.dt.uint16
@@ -27,10 +28,10 @@ def tile_som_kernel(tc, base, x, rate, offs, out):
         nc.sync.dma_start(x_sb[:], x.rearrange("(p r) c -> p r c", r=ROWS))
         rate_view = rate.rearrange("(p r) j -> p r j", r=ROWS)
         rate_sb = []
-        for pair in range(ROWS // 2):
-            rate_pair = held.tile([P, 2, N], BF16, name=f"rate{pair}")
-            nc.sync.dma_start(rate_pair[:], rate_view[:, 2 * pair : 2 * pair + 2, :])
-            rate_sb.append(rate_pair)
+        for g in range(ROWS // GROUP):
+            rate_group = held.tile([P, GROUP, N], BF16, name=f"rate{g}")
+            nc.sync.dma_start(rate_group[:], rate_view[:, g * GROUP : (g + 1) * GROUP, :])
+            rate_sb.append(rate_group)
 
         window = held.tile([P, S], F32, name="window")
         nc.sync.dma_start(window[:], base)
@@ -51,7 +52,7 @@ def tile_som_kernel(tc, base, x, rate, offs, out):
             nc.tensor.matmul(
                 num_ps[h][:],
                 x_sb[:, r, :],
-                rate_sb[r // 2][:, r % 2, h * BANK : (h + 1) * BANK],
+                rate_sb[r // GROUP][:, r % GROUP, h * BANK : (h + 1) * BANK],
                 start=(r == 0),
                 stop=(r == ROWS - 1),
             )
@@ -63,16 +64,18 @@ def tile_som_kernel(tc, base, x, rate, offs, out):
                     recip_ps[h][:, q * P : (q + 1) * P], recip_t[:, b : b + 1].to_broadcast([P, P]), identity[:]
                 )
 
-        for r in range(ROWS):
-            for b in range(BLOCKS):
-                nc.tensor.matmul(
-                    part_ps[:, b, r : r + 1],
-                    rate_sb[r // 2][:, r % 2, b * P : (b + 1) * P],
-                    one_col[:],
-                    start=True,
-                    stop=True,
-                )
-            add_to_num(0, r)
+        for g in range(ROWS // GROUP):
+            for r in range(g * GROUP, (g + 1) * GROUP):
+                for b in range(BLOCKS):
+                    nc.tensor.matmul(
+                        part_ps[:, b, r : r + 1],
+                        rate_sb[g][:, r % GROUP, b * P : (b + 1) * P],
+                        one_col[:],
+                        start=True,
+                        stop=True,
+                    )
+            for r in range(g * GROUP, (g + 1) * GROUP):
+                add_to_num(0, r)
 
         s_t = held.tile([P, BLOCKS], F32, name="s_t")
         nc.vector.reduce_sum(s_t[:], part_ps, axis=mybir.AxisListType.X)

@@ -9,6 +9,7 @@ BLOCKS = N // P
 BANK = 512
 HALVES = N // BANK
 BLOCKS_IN_HALF = BANK // P
+QUARTER = 256
 GROUP = 4
 FLOPS = 2 * P * N * N + N * N
 
@@ -44,7 +45,7 @@ def tile_som_kernel(tc, base, x, rate, offs, out):
         part_bank = psum.tile([P, BANK], F32, name="part_bank", tag="shared_bank")
         part_ps = part_bank[:, 0 : BLOCKS * ROWS].rearrange("p (b r) -> p b r", r=ROWS)
         num_ps = [psum.tile([P, BANK], F32, name="num_ps0")]
-        recip_ps = [psum.tile([P, BANK], F32, name=f"recip_ps{h}") for h in range(HALVES)]
+        recip_ps = [psum.tile([P, BANK], F32, name=f"recip_ps{k}") for k in range(N // QUARTER)]
         num = [held.tile([P, BANK], F32, name=f"num{h}") for h in range(HALVES)]
         recip = [held.tile([P, BANK], F32, name=f"recip{h}") for h in range(HALVES)]
 
@@ -57,12 +58,15 @@ def tile_som_kernel(tc, base, x, rate, offs, out):
                 stop=(r == ROWS - 1),
             )
 
-        def spread_recip(h):
-            for q in range(BLOCKS_IN_HALF):
-                b = h * BLOCKS_IN_HALF + q
-                nc.tensor.transpose(
-                    recip_ps[h][:, q * P : (q + 1) * P], recip_t[:, b : b + 1].to_broadcast([P, P]), identity[:]
-                )
+        def spread_recip(h, copy):
+            for k in range(h * BANK // QUARTER, (h + 1) * BANK // QUARTER):
+                for q in range(QUARTER // P):
+                    b = k * (QUARTER // P) + q
+                    nc.tensor.transpose(
+                        recip_ps[k][:, q * P : (q + 1) * P], recip_t[:, b : b + 1].to_broadcast([P, P]), identity[:]
+                    )
+                at = k * QUARTER - h * BANK
+                copy(recip[h][:, at : at + QUARTER], recip_ps[k][:, 0:QUARTER])
 
         for g in range(ROWS // GROUP):
             for r in range(g * GROUP, (g + 1) * GROUP):
@@ -83,11 +87,9 @@ def tile_som_kernel(tc, base, x, rate, offs, out):
         nc.vector.reciprocal(recip_t[:], s_t[:])
 
         nc.scalar.copy(num[0][:], num_ps[0][:])
-        spread_recip(0)
-        nc.vector.tensor_copy(recip[0][:], recip_ps[0][:])
+        spread_recip(0, nc.vector.tensor_copy)
 
-        spread_recip(1)
-        nc.scalar.copy(recip[1][:], recip_ps[1][:])
+        spread_recip(1, nc.scalar.copy)
         num_ps.append(psum.tile([P, BANK], F32, name="num_ps1", tag="shared_bank"))
         for r in range(ROWS):
             add_to_num(1, r)

@@ -5,15 +5,15 @@ P = 128
 S = 4096
 N = 1024
 ROWS = N // P
-BLOCKS = N // P
-BANK = 512
-HALVES = N // BANK
-BLOCKS_IN_HALF = BANK // P
-QUARTER = 256
-GROUP = 4
+EARLY = 4
+STEP = 2
+LAST = 7
+HALF = N // 2
+BLOCKS = HALF // P
 FLOPS = 2 * P * N * N + N * N
 
 BF16, F32, U16 = mybir.dt.bfloat16, mybir.dt.float32, mybir.dt.uint16
+ACT = mybir.ActivationFunctionType
 
 
 def tile_som_kernel(tc, base, x, rate, offs, out):
@@ -22,81 +22,97 @@ def tile_som_kernel(tc, base, x, rate, offs, out):
         tc.tile_pool(name="held", bufs=1) as held,
         tc.psum_pool(name="psum", bufs=1) as psum,
     ):
-        offsets = held.tile([P, N // 16], U16, name="offsets")
-        nc.sync.dma_start(offsets[:], offs)
+        rate_view = rate.rearrange("(p r) j -> p r j", r=ROWS)
+        pieces = []
+
+        def load_rate(r0, r1, j0, j1):
+            tile = held.tile([P, r1 - r0, j1 - j0], BF16, name=f"rate_{r0}_{j0}")
+            nc.sync.dma_start(tile[:], rate_view[:, r0:r1, j0:j1])
+            pieces.append((r0, r1, j0, j1, tile))
 
         x_sb = held.tile([P, ROWS, P], BF16, name="x_sb")
         nc.sync.dma_start(x_sb[:], x.rearrange("(p r) c -> p r c", r=ROWS))
-        rate_view = rate.rearrange("(p r) j -> p r j", r=ROWS)
-        rate_sb = []
-        for g in range(ROWS // GROUP):
-            rate_group = held.tile([P, GROUP, N], BF16, name=f"rate{g}")
-            nc.sync.dma_start(rate_group[:], rate_view[:, g * GROUP : (g + 1) * GROUP, :])
-            rate_sb.append(rate_group)
-
+        for r in range(0, EARLY, STEP):
+            load_rate(r, r + STEP, 0, N)
+        load_rate(EARLY, ROWS, 0, HALF)
+        offsets = held.tile([P, N // 16], U16, name="offsets")
+        nc.sync.dma_start(offsets[:], offs)
         window = held.tile([P, S], F32, name="window")
         nc.sync.dma_start(window[:], base)
+        load_rate(EARLY, LAST, HALF, N)
+        load_rate(LAST, ROWS, HALF, N)
 
         one_col = held.tile([P, 1], BF16, name="one_col")
         nc.vector.memset(one_col[:], 1.0)
+        zeros = held.tile([P, P], BF16, name="zeros")
+        nc.vector.memset(zeros[:], 0.0)
         identity = held.tile([P, P], F32, name="identity")
         make_identity(nc, identity[:])
 
-        part_bank = psum.tile([P, BANK], F32, name="part_bank", tag="shared_bank")
-        part_ps = part_bank[:, 0 : BLOCKS * ROWS].rearrange("p (b r) -> p b r", r=ROWS)
-        num_ps = [psum.tile([P, BANK], F32, name="num_ps0")]
-        recip_ps = [psum.tile([P, BANK], F32, name=f"recip_ps{k}") for k in range(N // QUARTER)]
-        num = [held.tile([P, BANK], F32, name=f"num{h}") for h in range(HALVES)]
-        recip = [held.tile([P, BANK], F32, name=f"recip{h}") for h in range(HALVES)]
+        def rate_row(h, r):
+            for r0, r1, j0, j1, tile in pieces:
+                if r0 <= r < r1 and j0 <= h * HALF < j1:
+                    return tile[:, r - r0, h * HALF - j0 : (h + 1) * HALF - j0]
 
-        def add_to_num(h, r):
-            nc.tensor.matmul(
-                num_ps[h][:],
-                x_sb[:, r, :],
-                rate_sb[r // GROUP][:, r % GROUP, h * BANK : (h + 1) * BANK],
-                start=(r == 0),
-                stop=(r == ROWS - 1),
-            )
+        def open_sums(s_ps):
+            nc.tensor.matmul(s_ps[:, 0:BLOCKS], zeros[:], zeros[:, 0:BLOCKS], start=True, stop=False)
 
-        def spread_recip(h, copy):
-            for k in range(h * BANK // QUARTER, (h + 1) * BANK // QUARTER):
-                for q in range(QUARTER // P):
-                    b = k * (QUARTER // P) + q
-                    nc.tensor.transpose(
-                        recip_ps[k][:, q * P : (q + 1) * P], recip_t[:, b : b + 1].to_broadcast([P, P]), identity[:]
-                    )
-                at = k * QUARTER - h * BANK
-                copy(recip[h][:, at : at + QUARTER], recip_ps[k][:, 0:QUARTER])
-
-        for g in range(ROWS // GROUP):
-            for r in range(g * GROUP, (g + 1) * GROUP):
+        def add_sums(s_ps, h, rows):
+            for r in rows:
                 for b in range(BLOCKS):
                     nc.tensor.matmul(
-                        part_ps[:, b, r : r + 1],
-                        rate_sb[g][:, r % GROUP, b * P : (b + 1) * P],
+                        s_ps[:, b : b + 1],
+                        rate_row(h, r)[:, b * P : (b + 1) * P],
                         one_col[:],
-                        start=True,
-                        stop=True,
+                        start=False,
+                        stop=(r == ROWS - 1 and b == BLOCKS - 1),
                     )
-            for r in range(g * GROUP, (g + 1) * GROUP):
-                add_to_num(0, r)
 
-        s_t = held.tile([P, BLOCKS], F32, name="s_t")
-        nc.vector.reduce_sum(s_t[:], part_ps, axis=mybir.AxisListType.X)
+        def add_num(num_ps, h, rows):
+            for r in rows:
+                nc.tensor.matmul(num_ps[:], x_sb[:, r, :], rate_row(h, r), start=(r == 0), stop=(r == ROWS - 1))
+
+        def spread(spread_ps, col_t):
+            for b in range(BLOCKS):
+                nc.tensor.transpose(
+                    spread_ps[:, b * P : (b + 1) * P], col_t[:, b : b + 1].to_broadcast([P, P]), identity[:]
+                )
+
+        s_ps = psum.tile([P, HALF], F32, name="s_ps0", tag="s_ps")
+        num_ps = psum.tile([P, HALF], F32, name="num_ps0", tag="num_ps")
+        spread_ps = psum.tile([P, HALF], F32, name="spread_ps0", tag="spread_ps")
+        num0 = held.tile([P, HALF], F32, name="num0")
+        recip0 = held.tile([P, HALF], F32, name="recip0")
         recip_t = held.tile([P, BLOCKS], F32, name="recip_t")
-        nc.vector.reciprocal(recip_t[:], s_t[:])
+        open_sums(s_ps)
+        for r in range(0, EARLY, STEP):
+            add_sums(s_ps, 0, range(r, r + STEP))
+            add_num(num_ps, 0, range(r, r + STEP))
+        add_sums(s_ps, 0, range(EARLY, ROWS))
+        nc.vector.reciprocal(recip_t[:], s_ps[:, 0:BLOCKS])
+        add_num(num_ps, 0, range(EARLY, ROWS))
+        spread(spread_ps, recip_t)
+        nc.vector.tensor_copy(recip0[:], spread_ps[:])
+        nc.vector.tensor_copy(num0[:], num_ps[:])
 
-        nc.scalar.copy(num[0][:], num_ps[0][:])
-        spread_recip(0, nc.vector.tensor_copy)
+        s_ps = psum.tile([P, HALF], F32, name="s_ps1", tag="s_ps")
+        num_ps = psum.tile([P, HALF], F32, name="num_ps1", tag="num_ps")
+        spread_ps = psum.tile([P, HALF], F32, name="spread_ps1", tag="spread_ps")
+        num1 = held.tile([P, HALF], F32, name="num1")
+        recip1 = held.tile([P, HALF], F32, name="recip1")
+        root_t = held.tile([P, BLOCKS], F32, name="root_t")
+        open_sums(s_ps)
+        add_sums(s_ps, 1, range(0, EARLY))
+        add_num(num_ps, 1, range(0, EARLY))
+        add_sums(s_ps, 1, range(EARLY, ROWS))
+        nc.scalar.activation(root_t[:], s_ps[:, 0:BLOCKS], ACT.Abs_reciprocal_sqrt)
+        add_num(num_ps, 1, range(EARLY, ROWS))
+        spread(spread_ps, root_t)
+        nc.scalar.square(recip1[:], spread_ps[:])
+        nc.scalar.copy(num1[:], num_ps[:])
 
-        spread_recip(1, nc.scalar.copy)
-        num_ps.append(psum.tile([P, BANK], F32, name="num_ps1", tag="shared_bank"))
-        for r in range(ROWS):
-            add_to_num(1, r)
-        nc.scalar.copy(num[1][:], num_ps[1][:])
-
-        for h in range(HALVES):
-            piece = offsets[:, h * (BANK // 16) : (h + 1) * (BANK // 16)]
-            nc.vector.tensor_tensor(window[:].indirect(piece), num[h][:], recip[h][:], mybir.AluOpType.mult)
+        for h, num, recip in ((0, num0, recip0), (1, num1, recip1)):
+            piece = offsets[:, h * (HALF // 16) : (h + 1) * (HALF // 16)]
+            nc.vector.tensor_tensor(window[:].indirect(piece), num[:], recip[:], mybir.AluOpType.mult)
 
         nc.sync.dma_start(out, window[:])

@@ -1,5 +1,4 @@
 import concourse.mybir as mybir
-from concourse.masks import make_identity
 
 P = 128
 S = 4096
@@ -7,13 +6,10 @@ N = 1024
 ROWS = N // P
 EARLY = 4
 STEP = 2
-LAST = 7
 HALF = N // 2
-BLOCKS = HALF // P
 FLOPS = 2 * P * N * N + N * N
 
 BF16, F32, U16 = mybir.dt.bfloat16, mybir.dt.float32, mybir.dt.uint16
-ACT = mybir.ActivationFunctionType
 
 
 def tile_som_kernel(tc, base, x, rate, offs, out):
@@ -26,9 +22,9 @@ def tile_som_kernel(tc, base, x, rate, offs, out):
         pieces = []
 
         def load_rate(r0, r1, j0, j1):
-            tile = held.tile([P, r1 - r0, j1 - j0], BF16, name=f"rate_{r0}_{j0}")
-            nc.sync.dma_start(tile[:], rate_view[:, r0:r1, j0:j1])
-            pieces.append((r0, r1, j0, j1, tile))
+            piece = held.tile([P, r1 - r0, j1 - j0], BF16, name=f"rate_{r0}_{j0}")
+            nc.sync.dma_start(piece[:], rate_view[:, r0:r1, j0:j1])
+            pieces.append((r0, r1, j0, j1, piece))
 
         x_sb = held.tile([P, ROWS, P], BF16, name="x_sb")
         nc.sync.dma_start(x_sb[:], x.rearrange("(p r) c -> p r c", r=ROWS))
@@ -39,80 +35,42 @@ def tile_som_kernel(tc, base, x, rate, offs, out):
         nc.sync.dma_start(offsets[:], offs)
         window = held.tile([P, S], F32, name="window")
         nc.sync.dma_start(window[:], base)
-        load_rate(EARLY, LAST, HALF, N)
-        load_rate(LAST, ROWS, HALF, N)
+        load_rate(EARLY, ROWS, HALF, N)
 
-        one_col = held.tile([P, 1], BF16, name="one_col")
-        nc.vector.memset(one_col[:], 1.0)
-        zeros = held.tile([P, P], BF16, name="zeros")
-        nc.vector.memset(zeros[:], 0.0)
-        identity = held.tile([P, P], F32, name="identity")
-        make_identity(nc, identity[:])
+        ones = held.tile([P, P], BF16, name="ones")
+        nc.vector.memset(ones[:], 1.0)
 
         def rate_row(h, r):
-            for r0, r1, j0, j1, tile in pieces:
+            for r0, r1, j0, j1, piece in pieces:
                 if r0 <= r < r1 and j0 <= h * HALF < j1:
-                    return tile[:, r - r0, h * HALF - j0 : (h + 1) * HALF - j0]
+                    return piece[:, r - r0, h * HALF - j0 : (h + 1) * HALF - j0]
 
-        def open_sums(s_ps):
-            nc.tensor.matmul(s_ps[:, 0:BLOCKS], zeros[:], zeros[:, 0:BLOCKS], start=True, stop=False)
-
-        def add_sums(s_ps, h, rows):
+        def add_rows(into_ps, weights, h, rows):
             for r in rows:
-                for b in range(BLOCKS):
-                    nc.tensor.matmul(
-                        s_ps[:, b : b + 1],
-                        rate_row(h, r)[:, b * P : (b + 1) * P],
-                        one_col[:],
-                        start=False,
-                        stop=(r == ROWS - 1 and b == BLOCKS - 1),
-                    )
+                nc.tensor.matmul(into_ps[:], weights(r), rate_row(h, r), start=(r == 0), stop=(r == ROWS - 1))
 
-        def add_num(num_ps, h, rows):
-            for r in rows:
-                nc.tensor.matmul(num_ps[:], x_sb[:, r, :], rate_row(h, r), start=(r == 0), stop=(r == ROWS - 1))
+        def x_row(r):
+            return x_sb[:, r, :]
 
-        def spread(spread_ps, col_t):
-            for b in range(BLOCKS):
-                nc.tensor.transpose(
-                    spread_ps[:, b * P : (b + 1) * P], col_t[:, b : b + 1].to_broadcast([P, P]), identity[:]
-                )
+        def all_ones(r):
+            return ones[:]
 
-        s_ps = psum.tile([P, HALF], F32, name="s_ps0", tag="s_ps")
-        num_ps = psum.tile([P, HALF], F32, name="num_ps0", tag="num_ps")
-        spread_ps = psum.tile([P, HALF], F32, name="spread_ps0", tag="spread_ps")
-        num0 = held.tile([P, HALF], F32, name="num0")
-        recip0 = held.tile([P, HALF], F32, name="recip0")
-        recip_t = held.tile([P, BLOCKS], F32, name="recip_t")
-        open_sums(s_ps)
-        for r in range(0, EARLY, STEP):
-            add_sums(s_ps, 0, range(r, r + STEP))
-            add_num(num_ps, 0, range(r, r + STEP))
-        add_sums(s_ps, 0, range(EARLY, ROWS))
-        nc.vector.reciprocal(recip_t[:], s_ps[:, 0:BLOCKS])
-        add_num(num_ps, 0, range(EARLY, ROWS))
-        spread(spread_ps, recip_t)
-        nc.vector.tensor_copy(recip0[:], spread_ps[:])
-        nc.vector.tensor_copy(num0[:], num_ps[:])
-
-        s_ps = psum.tile([P, HALF], F32, name="s_ps1", tag="s_ps")
-        num_ps = psum.tile([P, HALF], F32, name="num_ps1", tag="num_ps")
-        spread_ps = psum.tile([P, HALF], F32, name="spread_ps1", tag="spread_ps")
-        num1 = held.tile([P, HALF], F32, name="num1")
-        recip1 = held.tile([P, HALF], F32, name="recip1")
-        root_t = held.tile([P, BLOCKS], F32, name="root_t")
-        open_sums(s_ps)
-        add_sums(s_ps, 1, range(0, EARLY))
-        add_num(num_ps, 1, range(0, EARLY))
-        add_sums(s_ps, 1, range(EARLY, ROWS))
-        nc.scalar.activation(root_t[:], s_ps[:, 0:BLOCKS], ACT.Abs_reciprocal_sqrt)
-        add_num(num_ps, 1, range(EARLY, ROWS))
-        spread(spread_ps, root_t)
-        nc.scalar.square(recip1[:], spread_ps[:])
-        nc.scalar.copy(num1[:], num_ps[:])
-
-        for h, num, recip in ((0, num0, recip0), (1, num1, recip1)):
-            piece = offsets[:, h * (HALF // 16) : (h + 1) * (HALF // 16)]
-            nc.vector.tensor_tensor(window[:].indirect(piece), num[:], recip[:], mybir.AluOpType.mult)
+        for h, row_groups, copy in (
+            (0, ((0, 2), (2, 4), (4, 8)), nc.vector.tensor_copy),
+            (1, ((0, 4), (4, 8)), nc.scalar.copy),
+        ):
+            s_ps = psum.tile([P, HALF], F32, name=f"s_ps{h}", tag="s_ps")
+            num_ps = psum.tile([P, HALF], F32, name=f"num_ps{h}", tag="num_ps")
+            root = held.tile([P, HALF], F32, name=f"root{h}")
+            recip = held.tile([P, HALF], F32, name=f"recip{h}")
+            num = held.tile([P, HALF], F32, name=f"num{h}")
+            for r0, r1 in row_groups:
+                add_rows(s_ps, all_ones, h, range(r0, r1))
+                add_rows(num_ps, x_row, h, range(r0, r1))
+            nc.scalar.activation(root[:], s_ps[:], mybir.ActivationFunctionType.Abs_reciprocal_sqrt)
+            nc.scalar.square(recip[:], root[:])
+            copy(num[:], num_ps[:])
+            offsets_half = offsets[:, h * (HALF // 16) : (h + 1) * (HALF // 16)]
+            nc.vector.tensor_tensor(window[:].indirect(offsets_half), num[:], recip[:], mybir.AluOpType.mult)
 
         nc.sync.dma_start(out, window[:])

@@ -26,10 +26,10 @@ def tile_som_kernel(tc, base, x, rate, offs, out):
             nc.sync.dma_start(piece[:], rate_view[:, r0:r1, j0:j1])
             pieces.append((r0, r1, j0, j1, piece))
 
+        load_rate(0, STEP, 0, N)
         x_sb = held.tile([P, ROWS, P], BF16, name="x_sb")
         nc.sync.dma_start(x_sb[:], x.rearrange("(p r) c -> p r c", r=ROWS))
-        for r in range(0, EARLY, STEP):
-            load_rate(r, r + STEP, 0, N)
+        load_rate(STEP, EARLY, 0, N)
         load_rate(EARLY, ROWS, 0, HALF)
         offsets = held.tile([P, N // 16], U16, name="offsets")
         nc.sync.dma_start(offsets[:], offs)
@@ -59,8 +59,8 @@ def tile_som_kernel(tc, base, x, rate, offs, out):
             (0, ((0, 2), (2, 4), (4, 8)), nc.vector.tensor_copy),
             (1, ((0, 4), (4, 8)), nc.scalar.copy),
         ):
-            s_ps = psum.tile([P, HALF], F32, name=f"s_ps{h}", tag="s_ps")
-            num_ps = psum.tile([P, HALF], F32, name=f"num_ps{h}", tag="num_ps")
+            s_ps = psum.tile([P, HALF], F32, name=f"s_ps{h}")
+            num_ps = psum.tile([P, HALF], F32, name=f"num_ps{h}")
             root = held.tile([P, HALF], F32, name=f"root{h}")
             recip = held.tile([P, HALF], F32, name=f"recip{h}")
             num = held.tile([P, HALF], F32, name=f"num{h}")

@@ -4,8 +4,8 @@ P = 128
 S = 4096
 N = 1024
 ROWS = N // P
-EARLY = 4
 STEP = 2
+EARLY = 6
 HALF = N // 2
 FLOPS = 2 * P * N * N + N * N
 
@@ -21,56 +21,76 @@ def tile_som_kernel(tc, base, x, rate, offs, out):
         rate_view = rate.rearrange("(p r) j -> p r j", r=ROWS)
         pieces = []
 
-        def load_rate(r0, r1, j0, j1):
-            piece = held.tile([P, r1 - r0, j1 - j0], BF16, name=f"rate_{r0}_{j0}")
-            nc.sync.dma_start(piece[:], rate_view[:, r0:r1, j0:j1])
-            pieces.append((r0, r1, j0, j1, piece))
+        def load_rate(r0, j0, j1):
+            piece = held.tile([P, STEP, j1 - j0], BF16, name=f"rate_{r0}_{j0}")
+            nc.sync.dma_start(piece[:], rate_view[:, r0 : r0 + STEP, j0:j1])
+            pieces.append((r0, j0, j1, piece))
 
-        load_rate(0, STEP, 0, N)
+        load_rate(0, 0, N)
         x_sb = held.tile([P, ROWS, P], BF16, name="x_sb")
         nc.sync.dma_start(x_sb[:], x.rearrange("(p r) c -> p r c", r=ROWS))
-        load_rate(STEP, EARLY, 0, N)
-        load_rate(EARLY, ROWS, 0, HALF)
+        for r in range(STEP, EARLY, STEP):
+            load_rate(r, 0, N)
+        load_rate(EARLY, 0, HALF)
         offsets = held.tile([P, N // 16], U16, name="offsets")
         nc.sync.dma_start(offsets[:], offs)
         window = held.tile([P, S], F32, name="window")
         nc.sync.dma_start(window[:], base)
-        load_rate(EARLY, ROWS, HALF, N)
+        load_rate(EARLY, HALF, N)
 
         ones = held.tile([P, P], BF16, name="ones")
         nc.vector.memset(ones[:], 1.0)
 
+        s_ps = [psum.tile([P, HALF], F32, name=f"s_ps{h}") for h in range(2)]
+        num_ps = [psum.tile([P, HALF], F32, name=f"num_ps{h}") for h in range(2)]
+        root = [held.tile([P, HALF], F32, name=f"root{h}") for h in range(2)]
+        recip = [held.tile([P, HALF], F32, name=f"recip{h}") for h in range(2)]
+        num = [held.tile([P, HALF], F32, name=f"num{h}") for h in range(2)]
+
         def rate_row(h, r):
-            for r0, r1, j0, j1, piece in pieces:
-                if r0 <= r < r1 and j0 <= h * HALF < j1:
+            for r0, j0, j1, piece in pieces:
+                if r0 <= r < r0 + STEP and j0 <= h * HALF < j1:
                     return piece[:, r - r0, h * HALF - j0 : (h + 1) * HALF - j0]
 
-        def add_rows(into_ps, weights, h, rows):
+        def add_s(h, rows, start=False, stop=False):
             for r in rows:
-                nc.tensor.matmul(into_ps[:], weights(r), rate_row(h, r), start=(r == 0), stop=(r == ROWS - 1))
+                nc.tensor.matmul(
+                    s_ps[h][:], ones[:], rate_row(h, r), start=start and r == rows[0], stop=stop and r == rows[-1]
+                )
 
-        def x_row(r):
-            return x_sb[:, r, :]
+        def add_num(h, rows, start=False, stop=False):
+            for r in rows:
+                nc.tensor.matmul(
+                    num_ps[h][:], x_sb[:, r, :], rate_row(h, r), start=start and r == rows[0], stop=stop and r == rows[-1]
+                )
 
-        def all_ones(r):
-            return ones[:]
+        def take_recip(h):
+            nc.scalar.activation(root[h][:], s_ps[h][:], mybir.ActivationFunctionType.Abs_reciprocal_sqrt)
+            nc.scalar.square(recip[h][:], root[h][:])
 
-        for h, row_groups, copy in (
-            (0, ((0, 2), (2, 4), (4, 8)), nc.vector.tensor_copy),
-            (1, ((0, 4), (4, 8)), nc.scalar.copy),
-        ):
-            s_ps = psum.tile([P, HALF], F32, name=f"s_ps{h}")
-            num_ps = psum.tile([P, HALF], F32, name=f"num_ps{h}")
-            root = held.tile([P, HALF], F32, name=f"root{h}")
-            recip = held.tile([P, HALF], F32, name=f"recip{h}")
-            num = held.tile([P, HALF], F32, name=f"num{h}")
-            for r0, r1 in row_groups:
-                add_rows(s_ps, all_ones, h, range(r0, r1))
-                add_rows(num_ps, x_row, h, range(r0, r1))
-            nc.scalar.activation(root[:], s_ps[:], mybir.ActivationFunctionType.Abs_reciprocal_sqrt)
-            nc.scalar.square(recip[:], root[:])
-            copy(num[:], num_ps[:])
-            offsets_half = offsets[:, h * (HALF // 16) : (h + 1) * (HALF // 16)]
-            nc.vector.tensor_tensor(window[:].indirect(offsets_half), num[:], recip[:], mybir.AluOpType.mult)
+        def scatter(h):
+            piece = offsets[:, h * (HALF // 16) : (h + 1) * (HALF // 16)]
+            nc.vector.tensor_tensor(window[:].indirect(piece), num[h][:], recip[h][:], mybir.AluOpType.mult)
+
+        for r in range(0, ROWS, STEP):
+            rows = range(r, r + STEP)
+            add_s(0, rows, start=(r == 0), stop=(r + STEP == ROWS))
+            add_num(0, rows, start=(r == 0), stop=(r + STEP == ROWS))
+        take_recip(0)
+        nc.vector.tensor_copy(num[0][:], num_ps[0][:])
+        scatter(0)
+
+        newest = range(EARLY - STEP, EARLY)
+        oldest = range(0, EARLY - STEP)
+        late = range(EARLY, ROWS)
+        add_s(1, newest, start=True)
+        add_s(1, oldest)
+        add_num(1, newest, start=True)
+        add_s(1, late, stop=True)
+        take_recip(1)
+        add_num(1, late)
+        add_num(1, oldest, stop=True)
+        nc.scalar.copy(num[1][:], num_ps[1][:])
+        scatter(1)
 
         nc.sync.dma_start(out, window[:])

@@ -1,15 +1,18 @@
 import concourse.mybir as mybir
+from concourse.masks import make_identity
 
 P = 128
 S = 4096
 N = 1024
 ROWS = N // P
-STEP = 2
-EARLY = 6
+FIRST = 2
+EARLY = 5
 HALF = N // 2
+BLOCKS = HALF // P
 FLOPS = 2 * P * N * N + N * N
 
 BF16, F32, U16 = mybir.dt.bfloat16, mybir.dt.float32, mybir.dt.uint16
+RSQRT = mybir.ActivationFunctionType.Abs_reciprocal_sqrt
 
 
 def tile_som_kernel(tc, base, x, rate, offs, out):
@@ -21,42 +24,38 @@ def tile_som_kernel(tc, base, x, rate, offs, out):
         rate_view = rate.rearrange("(p r) j -> p r j", r=ROWS)
         pieces = []
 
-        def load_rate(r0, j0, j1):
-            piece = held.tile([P, STEP, j1 - j0], BF16, name=f"rate_{r0}_{j0}")
-            nc.sync.dma_start(piece[:], rate_view[:, r0 : r0 + STEP, j0:j1])
-            pieces.append((r0, j0, j1, piece))
+        def load_rate(r0, r1, j0, j1):
+            piece = held.tile([P, r1 - r0, j1 - j0], BF16, name=f"rate_{r0}_{j0}")
+            nc.sync.dma_start(piece[:], rate_view[:, r0:r1, j0:j1])
+            pieces.append((r0, r1, j0, j1, piece))
 
-        load_rate(0, 0, N)
+        load_rate(0, FIRST, 0, N)
         x_sb = held.tile([P, ROWS, P], BF16, name="x_sb")
         nc.sync.dma_start(x_sb[:], x.rearrange("(p r) c -> p r c", r=ROWS))
-        for r in range(STEP, EARLY, STEP):
-            load_rate(r, 0, N)
-        load_rate(EARLY, 0, HALF)
+        load_rate(FIRST, EARLY, 0, N)
+        load_rate(EARLY, ROWS, 0, HALF)
         offsets = held.tile([P, N // 16], U16, name="offsets")
         nc.sync.dma_start(offsets[:], offs)
         window = held.tile([P, S], F32, name="window")
         nc.sync.dma_start(window[:], base)
-        load_rate(EARLY, HALF, N)
+        load_rate(EARLY, ROWS, HALF, N)
 
         ones = held.tile([P, P], BF16, name="ones")
         nc.vector.memset(ones[:], 1.0)
+        zeros = held.tile([P, P], BF16, name="zeros")
+        nc.vector.memset(zeros[:], 0.0)
+        identity = held.tile([P, P], F32, name="identity")
+        make_identity(nc, identity[:])
 
         s_ps = [psum.tile([P, HALF], F32, name=f"s_ps{h}") for h in range(2)]
         num_ps = [psum.tile([P, HALF], F32, name=f"num_ps{h}") for h in range(2)]
-        root = [held.tile([P, HALF], F32, name=f"root{h}") for h in range(2)]
-        recip = [held.tile([P, HALF], F32, name=f"recip{h}") for h in range(2)]
         num = [held.tile([P, HALF], F32, name=f"num{h}") for h in range(2)]
+        recip = [held.tile([P, HALF], F32, name=f"recip{h}") for h in range(2)]
 
         def rate_row(h, r):
-            for r0, j0, j1, piece in pieces:
-                if r0 <= r < r0 + STEP and j0 <= h * HALF < j1:
+            for r0, r1, j0, j1, piece in pieces:
+                if r0 <= r < r1 and j0 <= h * HALF < j1:
                     return piece[:, r - r0, h * HALF - j0 : (h + 1) * HALF - j0]
-
-        def add_s(h, rows, start=False, stop=False):
-            for r in rows:
-                nc.tensor.matmul(
-                    s_ps[h][:], ones[:], rate_row(h, r), start=start and r == rows[0], stop=stop and r == rows[-1]
-                )
 
         def add_num(h, rows, start=False, stop=False):
             for r in rows:
@@ -64,33 +63,47 @@ def tile_som_kernel(tc, base, x, rate, offs, out):
                     num_ps[h][:], x_sb[:, r, :], rate_row(h, r), start=start and r == rows[0], stop=stop and r == rows[-1]
                 )
 
-        def take_recip(h):
-            nc.scalar.activation(root[h][:], s_ps[h][:], mybir.ActivationFunctionType.Abs_reciprocal_sqrt)
-            nc.scalar.square(recip[h][:], root[h][:])
-
         def scatter(h):
             piece = offsets[:, h * (HALF // 16) : (h + 1) * (HALF // 16)]
             nc.vector.tensor_tensor(window[:].indirect(piece), num[h][:], recip[h][:], mybir.AluOpType.mult)
 
-        for r in range(0, ROWS, STEP):
-            rows = range(r, r + STEP)
-            add_s(0, rows, start=(r == 0), stop=(r + STEP == ROWS))
-            add_num(0, rows, start=(r == 0), stop=(r + STEP == ROWS))
-        take_recip(0)
+        first, middle, late = range(0, FIRST), range(FIRST, EARLY), range(EARLY, ROWS)
+
+        for rows in (first, middle, late):
+            for r in rows:
+                nc.tensor.matmul(s_ps[0][:], ones[:], rate_row(0, r), start=(r == 0), stop=(r == ROWS - 1))
+            add_num(0, rows, start=(rows == first), stop=(rows == late))
+        root = held.tile([P, HALF], F32, name="root")
+        nc.scalar.activation(root[:], s_ps[0][:], RSQRT)
+        nc.scalar.square(recip[0][:], root[:])
         nc.vector.tensor_copy(num[0][:], num_ps[0][:])
         scatter(0)
 
-        newest = range(EARLY - STEP, EARLY)
-        oldest = range(0, EARLY - STEP)
-        late = range(EARLY, ROWS)
-        add_s(1, newest, start=True)
-        add_s(1, oldest)
-        add_num(1, newest, start=True)
-        add_s(1, late, stop=True)
-        take_recip(1)
-        add_num(1, late)
-        add_num(1, oldest, stop=True)
+        def add_s_blocks(rows, stop=False):
+            for r in rows:
+                for b in range(BLOCKS):
+                    nc.tensor.matmul(
+                        s_ps[1][:, b : b + 1],
+                        rate_row(1, r)[:, b * P : (b + 1) * P],
+                        ones[:, 0:1],
+                        start=False,
+                        stop=stop and r == rows[-1] and b == BLOCKS - 1,
+                    )
+
+        nc.tensor.matmul(s_ps[1][:, 0:BLOCKS], zeros[:], zeros[:, 0:BLOCKS], start=True, stop=False)
+        add_s_blocks(middle)
+        add_s_blocks(first)
+        add_num(1, middle, start=True)
+        add_num(1, first)
+        add_s_blocks(late, stop=True)
+        root_t = held.tile([P, BLOCKS], F32, name="root_t")
+        nc.scalar.activation(root_t[:], s_ps[1][:, 0:BLOCKS], RSQRT)
+        add_num(1, late, stop=True)
         nc.scalar.copy(num[1][:], num_ps[1][:])
+        root_ps = psum.tile([P, HALF], F32, name="root_ps")
+        for b in range(BLOCKS):
+            nc.tensor.transpose(root_ps[:, b * P : (b + 1) * P], root_t[:, b : b + 1].to_broadcast([P, P]), identity[:])
+        nc.scalar.square(recip[1][:], root_ps[:])
         scatter(1)
 
         nc.sync.dma_start(out, window[:])

@@ -6,9 +6,10 @@ S = 4096
 N = 1024
 ROWS = N // P
 FIRST = 2
-EARLY = 5
+EARLY = 4
 HALF = N // 2
 BLOCKS = HALF // P
+QUARTER = HALF // 2
 FLOPS = 2 * P * N * N + N * N
 
 BF16, F32, U16 = mybir.dt.bfloat16, mybir.dt.float32, mybir.dt.uint16
@@ -47,8 +48,8 @@ def tile_som_kernel(tc, base, x, rate, offs, out):
         identity = held.tile([P, P], F32, name="identity")
         make_identity(nc, identity[:])
 
-        s_ps = [psum.tile([P, HALF], F32, name=f"s_ps{h}") for h in range(2)]
-        num_ps = [psum.tile([P, HALF], F32, name=f"num_ps{h}") for h in range(2)]
+        s_ps = psum.tile([P, HALF], F32, name="s_ps", tag="s_ps")
+        num_ps = psum.tile([P, HALF], F32, name="num_ps", tag="num_ps")
         num = [held.tile([P, HALF], F32, name=f"num{h}") for h in range(2)]
         recip = [held.tile([P, HALF], F32, name=f"recip{h}") for h in range(2)]
 
@@ -57,10 +58,10 @@ def tile_som_kernel(tc, base, x, rate, offs, out):
                 if r0 <= r < r1 and j0 <= h * HALF < j1:
                     return piece[:, r - r0, h * HALF - j0 : (h + 1) * HALF - j0]
 
-        def add_num(h, rows, start=False, stop=False):
+        def add_num(into_ps, rate_of_row, rows, start=False, stop=False):
             for r in rows:
                 nc.tensor.matmul(
-                    num_ps[h][:], x_sb[:, r, :], rate_row(h, r), start=start and r == rows[0], stop=stop and r == rows[-1]
+                    into_ps, x_sb[:, r, :], rate_of_row(r), start=start and r == rows[0], stop=stop and r == rows[-1]
                 )
 
         def scatter(h):
@@ -69,41 +70,64 @@ def tile_som_kernel(tc, base, x, rate, offs, out):
 
         first, middle, late = range(0, FIRST), range(FIRST, EARLY), range(EARLY, ROWS)
 
-        for rows in (first, middle, late):
+        def add_s(rows):
             for r in rows:
-                nc.tensor.matmul(s_ps[0][:], ones[:], rate_row(0, r), start=(r == 0), stop=(r == ROWS - 1))
-            add_num(0, rows, start=(rows == first), stop=(rows == late))
+                nc.tensor.matmul(s_ps[:], ones[:], rate_row(0, r), start=(r == 0), stop=(r == ROWS - 1))
+
+        def half_of_row(r):
+            return rate_row(0, r)
+
+        add_s(first)
+        add_num(num_ps[:], half_of_row, first, start=True)
+        add_s(middle)
+        add_s(late)
         root = held.tile([P, HALF], F32, name="root")
-        nc.scalar.activation(root[:], s_ps[0][:], RSQRT)
-        nc.scalar.square(recip[0][:], root[:])
-        nc.vector.tensor_copy(num[0][:], num_ps[0][:])
+        nc.scalar.activation(root[:], s_ps[:], RSQRT)
+        nc.vector.tensor_mul(recip[0][:], root[:], root[:])
+        add_num(num_ps[:], half_of_row, middle)
+        add_num(num_ps[:], half_of_row, late, stop=True)
+        nc.scalar.copy(num[0][:], num_ps[:])
         scatter(0)
+
+        s_blocks_ps = psum.tile([P, HALF], F32, name="s_blocks_ps", tag="s_ps")
+        quarter_ps = [
+            psum.tile([P, HALF], F32, name="quarter_ps0", tag="num_ps"),
+            psum.tile([P, HALF], F32, name="quarter_ps1"),
+        ]
 
         def add_s_blocks(rows, stop=False):
             for r in rows:
                 for b in range(BLOCKS):
                     nc.tensor.matmul(
-                        s_ps[1][:, b : b + 1],
+                        s_blocks_ps[:, b : b + 1],
                         rate_row(1, r)[:, b * P : (b + 1) * P],
                         ones[:, 0:1],
                         start=False,
                         stop=stop and r == rows[-1] and b == BLOCKS - 1,
                     )
 
-        nc.tensor.matmul(s_ps[1][:, 0:BLOCKS], zeros[:], zeros[:, 0:BLOCKS], start=True, stop=False)
+        nc.tensor.matmul(s_blocks_ps[:, 0:BLOCKS], zeros[:], zeros[:, 0:BLOCKS], start=True, stop=False)
+        def quarter_of_row(k):
+            return lambda r: rate_row(1, r)[:, k * QUARTER : (k + 1) * QUARTER]
+
         add_s_blocks(middle)
         add_s_blocks(first)
-        add_num(1, middle, start=True)
-        add_num(1, first)
+        for k in range(2):
+            add_num(quarter_ps[k][:, 0:QUARTER], quarter_of_row(k), middle, start=True)
+            add_num(quarter_ps[k][:, 0:QUARTER], quarter_of_row(k), first)
         add_s_blocks(late, stop=True)
         root_t = held.tile([P, BLOCKS], F32, name="root_t")
-        nc.scalar.activation(root_t[:], s_ps[1][:, 0:BLOCKS], RSQRT)
-        add_num(1, late, stop=True)
-        nc.scalar.copy(num[1][:], num_ps[1][:])
+        nc.scalar.activation(root_t[:], s_blocks_ps[:, 0:BLOCKS], RSQRT)
+        def finish_quarter(k):
+            add_num(quarter_ps[k][:, 0:QUARTER], quarter_of_row(k), late, stop=True)
+            nc.scalar.copy(num[1][:, k * QUARTER : (k + 1) * QUARTER], quarter_ps[k][:, 0:QUARTER])
+
+        finish_quarter(0)
         root_ps = psum.tile([P, HALF], F32, name="root_ps")
         for b in range(BLOCKS):
             nc.tensor.transpose(root_ps[:, b * P : (b + 1) * P], root_t[:, b : b + 1].to_broadcast([P, P]), identity[:])
         nc.scalar.square(recip[1][:], root_ps[:])
+        finish_quarter(1)
         scatter(1)
 
         nc.sync.dma_start(out, window[:])

@@ -8,8 +8,8 @@ ROWS = N // P
 FIRST = 2
 EARLY = 4
 HALF = N // 2
-BLOCKS = HALF // P
 QUARTER = HALF // 2
+BLOCKS = HALF // P
 FLOPS = 2 * P * N * N + N * N
 
 BF16, F32, U16 = mybir.dt.bfloat16, mybir.dt.float32, mybir.dt.uint16
@@ -48,21 +48,28 @@ def tile_som_kernel(tc, base, x, rate, offs, out):
         identity = held.tile([P, P], F32, name="identity")
         make_identity(nc, identity[:])
 
-        s_ps = psum.tile([P, HALF], F32, name="s_ps", tag="s_ps")
-        num_ps = psum.tile([P, HALF], F32, name="num_ps", tag="num_ps")
         num = [held.tile([P, HALF], F32, name=f"num{h}") for h in range(2)]
         recip = [held.tile([P, HALF], F32, name=f"recip{h}") for h in range(2)]
+        s_ps = psum.tile([P, HALF], F32, name="s_ps", tag="s_ps")
+        num_ps = [psum.tile([P, HALF], F32, name=f"num_ps0_{k}", tag=f"num_ps{k}") for k in range(2)]
 
         def rate_row(h, r):
             for r0, r1, j0, j1, piece in pieces:
                 if r0 <= r < r1 and j0 <= h * HALF < j1:
                     return piece[:, r - r0, h * HALF - j0 : (h + 1) * HALF - j0]
 
-        def add_num(into_ps, rate_of_row, rows, start=False, stop=False):
+        def add_num(h, k, rows, start=False, stop=False):
             for r in rows:
                 nc.tensor.matmul(
-                    into_ps, x_sb[:, r, :], rate_of_row(r), start=start and r == rows[0], stop=stop and r == rows[-1]
+                    num_ps[k][:, 0:QUARTER],
+                    x_sb[:, r, :],
+                    rate_row(h, r)[:, k * QUARTER : (k + 1) * QUARTER],
+                    start=start and r == rows[0],
+                    stop=stop and r == rows[-1],
                 )
+
+        def copy_num(h, k):
+            nc.scalar.copy(num[h][:, k * QUARTER : (k + 1) * QUARTER], num_ps[k][:, 0:QUARTER])
 
         def scatter(h):
             piece = offsets[:, h * (HALF // 16) : (h + 1) * (HALF // 16)]
@@ -74,26 +81,22 @@ def tile_som_kernel(tc, base, x, rate, offs, out):
             for r in rows:
                 nc.tensor.matmul(s_ps[:], ones[:], rate_row(0, r), start=(r == 0), stop=(r == ROWS - 1))
 
-        def half_of_row(r):
-            return rate_row(0, r)
-
         add_s(first)
-        add_num(num_ps[:], half_of_row, first, start=True)
+        for k in range(2):
+            add_num(0, k, first, start=True)
         add_s(middle)
         add_s(late)
         root = held.tile([P, HALF], F32, name="root")
         nc.scalar.activation(root[:], s_ps[:], RSQRT)
         nc.vector.tensor_mul(recip[0][:], root[:], root[:])
-        add_num(num_ps[:], half_of_row, middle)
-        add_num(num_ps[:], half_of_row, late, stop=True)
-        nc.scalar.copy(num[0][:], num_ps[:])
+        for k in range(2):
+            add_num(0, k, late)
+            add_num(0, k, middle, stop=True)
+            copy_num(0, k)
         scatter(0)
 
         s_blocks_ps = psum.tile([P, HALF], F32, name="s_blocks_ps", tag="s_ps")
-        quarter_ps = [
-            psum.tile([P, HALF], F32, name="quarter_ps0", tag="num_ps"),
-            psum.tile([P, HALF], F32, name="quarter_ps1"),
-        ]
+        num_ps = [psum.tile([P, HALF], F32, name=f"num_ps1_{k}", tag=f"num_ps{k}") for k in range(2)]
 
         def add_s_blocks(rows, stop=False):
             for r in rows:
@@ -107,27 +110,22 @@ def tile_som_kernel(tc, base, x, rate, offs, out):
                     )
 
         nc.tensor.matmul(s_blocks_ps[:, 0:BLOCKS], zeros[:], zeros[:, 0:BLOCKS], start=True, stop=False)
-        def quarter_of_row(k):
-            return lambda r: rate_row(1, r)[:, k * QUARTER : (k + 1) * QUARTER]
-
-        add_s_blocks(middle)
         add_s_blocks(first)
+        add_s_blocks(middle)
         for k in range(2):
-            add_num(quarter_ps[k][:, 0:QUARTER], quarter_of_row(k), middle, start=True)
-            add_num(quarter_ps[k][:, 0:QUARTER], quarter_of_row(k), first)
+            add_num(1, k, first, start=True)
+            add_num(1, k, middle)
         add_s_blocks(late, stop=True)
         root_t = held.tile([P, BLOCKS], F32, name="root_t")
         nc.scalar.activation(root_t[:], s_blocks_ps[:, 0:BLOCKS], RSQRT)
-        def finish_quarter(k):
-            add_num(quarter_ps[k][:, 0:QUARTER], quarter_of_row(k), late, stop=True)
-            nc.scalar.copy(num[1][:, k * QUARTER : (k + 1) * QUARTER], quarter_ps[k][:, 0:QUARTER])
-
-        finish_quarter(0)
+        add_num(1, 0, late, stop=True)
+        copy_num(1, 0)
         root_ps = psum.tile([P, HALF], F32, name="root_ps")
         for b in range(BLOCKS):
             nc.tensor.transpose(root_ps[:, b * P : (b + 1) * P], root_t[:, b : b + 1].to_broadcast([P, P]), identity[:])
         nc.scalar.square(recip[1][:], root_ps[:])
-        finish_quarter(1)
+        add_num(1, 1, late, stop=True)
+        copy_num(1, 1)
         scatter(1)
 
         nc.sync.dma_start(out, window[:])

@@ -6,7 +6,7 @@ S = 4096
 N = 1024
 ROWS = N // P
 FIRST = 2
-EARLY = 4
+EARLY = 5
 HALF = N // 2
 QUARTER = HALF // 2
 BLOCKS = HALF // P

import concourse.mybir as mybir
from concourse.masks import make_identity

P = 128
S = 4096
N = 1024
ROWS = N // P
FIRST = 2
EARLY = 5
HALF = N // 2
QUARTER = HALF // 2
BLOCKS = HALF // P
FLOPS = 2 * P * N * N + N * N

BF16, F32, U16 = mybir.dt.bfloat16, mybir.dt.float32, mybir.dt.uint16
RSQRT = mybir.ActivationFunctionType.Abs_reciprocal_sqrt


def tile_som_kernel(tc, base, x, rate, offs, out):
    nc = tc.nc
    with (
        tc.tile_pool(name="held", bufs=1) as held,
        tc.psum_pool(name="psum", bufs=1) as psum,
    ):
        rate_view = rate.rearrange("(p r) j -> p r j", r=ROWS)
        pieces = []

        def load_rate(r0, r1, j0, j1):
            piece = held.tile([P, r1 - r0, j1 - j0], BF16, name=f"rate_{r0}_{j0}")
            nc.sync.dma_start(piece[:], rate_view[:, r0:r1, j0:j1])
            pieces.append((r0, r1, j0, j1, piece))

        load_rate(0, FIRST, 0, N)
        x_sb = held.tile([P, ROWS, P], BF16, name="x_sb")
        nc.sync.dma_start(x_sb[:], x.rearrange("(p r) c -> p r c", r=ROWS))
        load_rate(FIRST, EARLY, 0, N)
        load_rate(EARLY, ROWS, 0, HALF)
        offsets = held.tile([P, N // 16], U16, name="offsets")
        nc.sync.dma_start(offsets[:], offs)
        window = held.tile([P, S], F32, name="window")
        nc.sync.dma_start(window[:], base)
        load_rate(EARLY, ROWS, HALF, N)

        ones = held.tile([P, P], BF16, name="ones")
        nc.vector.memset(ones[:], 1.0)
        zeros = held.tile([P, P], BF16, name="zeros")
        nc.vector.memset(zeros[:], 0.0)
        identity = held.tile([P, P], F32, name="identity")
        make_identity(nc, identity[:])

        num = [held.tile([P, HALF], F32, name=f"num{h}") for h in range(2)]
        recip = [held.tile([P, HALF], F32, name=f"recip{h}") for h in range(2)]
        s_ps = psum.tile([P, HALF], F32, name="s_ps", tag="s_ps")
        num_ps = [psum.tile([P, HALF], F32, name=f"num_ps0_{k}", tag=f"num_ps{k}") for k in range(2)]

        def rate_row(h, r):
            for r0, r1, j0, j1, piece in pieces:
                if r0 <= r < r1 and j0 <= h * HALF < j1:
                    return piece[:, r - r0, h * HALF - j0 : (h + 1) * HALF - j0]

        def add_num(h, k, rows, start=False, stop=False):
            for r in rows:
                nc.tensor.matmul(
                    num_ps[k][:, 0:QUARTER],
                    x_sb[:, r, :],
                    rate_row(h, r)[:, k * QUARTER : (k + 1) * QUARTER],
                    start=start and r == rows[0],
                    stop=stop and r == rows[-1],
                )

        def copy_num(h, k):
            nc.scalar.copy(num[h][:, k * QUARTER : (k + 1) * QUARTER], num_ps[k][:, 0:QUARTER])

        def scatter(h):
            piece = offsets[:, h * (HALF // 16) : (h + 1) * (HALF // 16)]
            nc.vector.tensor_tensor(window[:].indirect(piece), num[h][:], recip[h][:], mybir.AluOpType.mult)

        first, middle, late = range(0, FIRST), range(FIRST, EARLY), range(EARLY, ROWS)

        def add_s(rows):
            for r in rows:
                nc.tensor.matmul(s_ps[:], ones[:], rate_row(0, r), start=(r == 0), stop=(r == ROWS - 1))

        add_s(first)
        for k in range(2):
            add_num(0, k, first, start=True)
        add_s(middle)
        add_s(late)
        root = held.tile([P, HALF], F32, name="root")
        nc.scalar.activation(root[:], s_ps[:], RSQRT)
        nc.vector.tensor_mul(recip[0][:], root[:], root[:])
        for k in range(2):
            add_num(0, k, late)
            add_num(0, k, middle, stop=True)
            copy_num(0, k)
        scatter(0)

        s_blocks_ps = psum.tile([P, HALF], F32, name="s_blocks_ps", tag="s_ps")
        num_ps = [psum.tile([P, HALF], F32, name=f"num_ps1_{k}", tag=f"num_ps{k}") for k in range(2)]

        def add_s_blocks(rows, stop=False):
            for r in rows:
                for b in range(BLOCKS):
                    nc.tensor.matmul(
                        s_blocks_ps[:, b : b + 1],
                        rate_row(1, r)[:, b * P : (b + 1) * P],
                        ones[:, 0:1],
                        start=False,
                        stop=stop and r == rows[-1] and b == BLOCKS - 1,
                    )

        nc.tensor.matmul(s_blocks_ps[:, 0:BLOCKS], zeros[:], zeros[:, 0:BLOCKS], start=True, stop=False)
        add_s_blocks(first)
        add_s_blocks(middle)
        for k in range(2):
            add_num(1, k, first, start=True)
            add_num(1, k, middle)
        add_s_blocks(late, stop=True)
        root_t = held.tile([P, BLOCKS], F32, name="root_t")
        nc.scalar.activation(root_t[:], s_blocks_ps[:, 0:BLOCKS], RSQRT)
        add_num(1, 0, late, stop=True)
        copy_num(1, 0)
        root_ps = psum.tile([P, HALF], F32, name="root_ps")
        for b in range(BLOCKS):
            nc.tensor.transpose(root_ps[:, b * P : (b + 1) * P], root_t[:, b : b + 1].to_broadcast([P, P]), identity[:])
        nc.scalar.square(recip[1][:], root_ps[:])
        add_num(1, 1, late, stop=True)
        copy_num(1, 1)
        scatter(1)

        nc.sync.dma_start(out, window[:])
